import numpy as np
import ml_dtypes


def mxq(x, axis, fmt="e4m3"):
    dtype, down = {"e4m3": (ml_dtypes.float8_e4m3fn, 7), "e5m2": (ml_dtypes.float8_e5m2, 14)}[fmt]
    v = np.moveaxis(np.asarray(x, np.float32).astype(ml_dtypes.bfloat16).astype(np.float64), axis, -1)
    blocks = v.reshape(v.shape[:-1] + (-1, 32))
    amax = np.abs(blocks).max(-1, keepdims=True)
    byte = np.maximum(np.where(amax > 0, np.frexp(amax)[1] - 1 + 127, 0) - down, 1)
    scale = np.exp2(byte - 127.0)
    codes = (blocks / scale).astype(np.float32).astype(dtype).astype(np.float64)
    return np.moveaxis((codes * scale).reshape(v.shape), -1, axis)


WIDE = False


def mx_kscale(k):
    if not WIDE:
        return np.ones(k)
    levels = np.array([10, -10, 5, -5, 0])
    if k % 512:
        return np.exp2(np.random.permutation(np.resize(levels, k // 32))).repeat(32)
    a = np.empty((k // 512, 16))
    for p in range(k // 512):
        a[p, :8] = np.random.permutation(np.resize(levels, 8))
        for g in range(8):
            far = levels[np.abs(levels - a[p, g]) >= 10]
            a[p, g + 8] = far[np.random.randint(len(far))]
    return np.exp2(a.ravel()).repeat(32)


BF16 = ml_dtypes.bfloat16


def bf(x):
    return np.asarray(x, np.float32).astype(BF16)


def f64(x):
    return np.asarray(x).astype(np.float64)


B, S, D, H, DH, DR, DKV, DQ = 1, 4096, 4096, 16, 128, 64, 1024, 2048
HALF = DR // 2


def rope(t, cos, sin):
    t1, t2 = t[..., 0::2], t[..., 1::2]
    c = cos[None, :, None, :]
    s = sin[None, :, None, :]
    return np.stack([t1 * c - t2 * s, t1 * s + t2 * c], axis=-1).reshape(t.shape)


def setup_inputs():
    s, t = mx_kscale(D), mx_kscale(DQ)
    ang = np.random.uniform(0.0, 2.0 * np.pi, (S, HALF))
    return {"x": bf(np.random.standard_normal((B, S, D)) * s),
            "W_q_down": bf(np.random.standard_normal((D, DQ)) / np.sqrt(D) / s[:, None] * t),
            "W_q_up": bf(np.random.standard_normal((DQ, H * DH)) / np.sqrt(DQ) / t[:, None]),
            "W_q_rope": bf(np.random.standard_normal((DQ, H * DR)) / np.sqrt(DQ) / t[:, None]),
            "rope_cos": bf(np.cos(ang)), "rope_sin": bf(np.sin(ang))}


def reference(x, W_q_down, W_q_up, W_q_rope, rope_cos, rope_sin):
    down_q = mxq(f64(x), 2, "e4m3") @ mxq(f64(W_q_down), 0, "e4m3")
    dq = mxq(down_q, 2, "e4m3")
    q_c = (dq @ mxq(f64(W_q_up), 0, "e4m3")).reshape(B, S, H, DH)
    q_r = (dq @ mxq(f64(W_q_rope), 0, "e4m3")).reshape(B, S, H, DR)
    q_r = rope(q_r, f64(rope_cos), f64(rope_sin))
    return np.concatenate([q_c, q_r], axis=-1).transpose(0, 2, 1, 3)

@@ -1,0 +1,425 @@
+from contextlib import ExitStack
+
+import concourse.mybir as mybir
+from concourse.masks import make_identity
+
+F32 = mybir.dt.float32
+BF16 = mybir.dt.bfloat16
+U32 = mybir.dt.uint32
+U8 = mybir.dt.uint8
+FP8X4 = mybir.dt.float8_e4m3fn_x4
+ALU = mybir.AluOpType
+
+P = 128
+S, D, DQ = 4096, 4096, 2048
+H, DH, DR = 16, 128, 64
+HALF = DR // 2
+NT = S // P
+NB = 8
+G1 = D // 512
+G2 = DQ // 512
+FLOPS = 2 * S * D * DQ + 2 * S * DQ * (H * DH + H * DR)
+
+
+def build(tc, x, W_q_down, W_q_up, W_q_rope, rope_cos, rope_sin, out, ctx, cfg):
+    nc = tc.nc
+    ctx.enter_context(tc.manual_schedule())
+    const = ctx.enter_context(tc.tile_pool(name="const", bufs=1))
+    wpool = ctx.enter_context(tc.tile_pool(name="wts", bufs=1))
+    act = ctx.enter_context(tc.tile_pool(name="act", bufs=2))
+    late = ctx.enter_context(tc.tile_pool(name="late", bufs=2))
+    psum = ctx.enter_context(tc.psum_pool(name="psum", bufs=4))
+
+    xv = x[0].rearrange("(p n) d -> p n d", n=NT)
+    ov = out[0].rearrange("h (p n) f -> n p h f", n=NT)
+    st = {}
+
+    def setup():
+        ident = const.tile([P, P], F32, name="ident", tag="ident")
+        make_identity(nc, ident[:])
+        st["ident"] = ident
+
+    def tables():
+        cos = const.tile([P, NT, HALF], BF16, name="cos", tag="cos")
+        sin = const.tile([P, NT, HALF], BF16, name="sin", tag="sin")
+        nc.sync.dma_start(out=cos[:], in_=rope_cos.rearrange("(p n) i -> p n i", n=NT))
+        nc.sync.dma_start(out=sin[:], in_=rope_sin.rearrange("(p n) i -> p n i", n=NT))
+        st["cos"], st["sin"] = cos, sin
+
+    def w_src(u):
+        kind, c, g = u
+        if kind == "down":
+            w = W_q_down[512 * g:512 * (g + 1), 512 * c:512 * (c + 1)]
+        elif c < 4:
+            w = W_q_up[512 * g:512 * (g + 1), 512 * c:512 * (c + 1)]
+        else:
+            w = W_q_rope[512 * g:512 * (g + 1), 512 * (c - 4):512 * (c - 3)]
+        return w.rearrange("(p j) w -> p j w", j=4)
+
+    def w_load(pi, ua, ub):
+        tg = ("up0c0", "up1c0", "up4c0", "up2c0", "wraw", "wraw")[pi % 6] if pi < 16 else "wraw"
+        if tg == "wraw":
+            wr = late.tile([P, 2, 4, 512], BF16, name="wraw", tag="wraw", bufs=2, offset=0)
+        else:
+            wr = wpool.tile([P, 2, 4, 512], BF16, name=tg, tag=tg, align_bytes=64)
+        nc.sync.dma_start(out=wr[:, 0], in_=w_src(ua))
+        nc.sync.dma_start(out=wr[:, 1], in_=w_src(ub))
+        st[("wraw", ua)] = wr[:, 0]
+        st[("wraw", ub)] = wr[:, 1]
+
+    def w_inter(u, eng):
+        kind, c, g = u
+        wr = st.pop(("wraw", u))
+        gr = act.tile([P, 2048], BF16, name="grp", tag="grp", bufs=cfg["grp_bufs"], align_bytes=64)
+        cp = eng.tensor_copy if eng is nc.vector else eng.copy
+        if kind == "down":
+            cp(out=gr[:].rearrange("p (t m j) -> p t m j", t=4, j=4), in_=wr.rearrange("p j (m t) -> p t m j", t=4))
+        elif c < 4:
+            cp(out=gr[:].rearrange("p (w j) -> p w j", j=4), in_=wr.rearrange("p j w -> p w j"))
+        else:
+            go = gr[:].rearrange("p (h e i j) -> p h e i j", h=8, e=2, j=4)
+            wi = wr.rearrange("p j (h i e) -> p h e i j", h=8, e=2)
+            for e in range(2):
+                cp(out=go[:, :, e], in_=wi[:, :, e])
+        st[("wgrp", u)] = gr
+
+    def w_codes(u):
+        kind, c, g = u
+        key = (kind, c)
+        if key not in st:
+            ng = G1 if kind == "down" else G2
+            nm = "%s%d" % (kind, c)
+            st[key] = [wpool.tile([P, 4, 512], U32, name="%sc%d" % (nm, q), tag="%sc%d" % (nm, q), align_bytes=64) for q in range(ng // 4)]
+            st[(kind, c, "pl")] = [wpool.tile([P, 512], U8, name="%sp%d" % (nm, q), tag="%sp%d" % (nm, q), align_bytes=64) for q in range(ng // 4)]
+        return st[key][g // 4][:, g % 4, :], st[(kind, c, "pl")][g // 4][4 * (g % 4):P, :]
+
+    def w_quant(u):
+        gr = st.pop(("wgrp", u))
+        cd, pl = w_codes(u)
+        nc.vector.quantize_mx(out=cd.bitcast(FP8X4), scales=pl, in_=gr[:])
+
+    def x_load(q):
+        b, r = q // 4, q % 4
+        tg = ("raw", "raw", "xs", "dqc")[q % 4] if q < 8 else ("xs" if q == 10 else "raw")
+        if tg == "raw":
+            raw = act.tile([P, 4, 1024], BF16, name="raw", tag="raw", bufs=2)
+        elif tg == "xs":
+            raw = act.tile([P, 4, 1024], BF16, name="xs", tag="xs", bufs=1)
+        else:
+            raw = act.tile([P, 4, 1024], BF16, name="dqc", tag="dqc", bufs=cfg["dq_bufs"], align_bytes=64)
+        nc.sync.dma_start(out=raw[:], in_=xv[:, 4 * b:4 * b + 4, 1024 * r:1024 * (r + 1)])
+        st[("raw", q)] = raw
+
+    def x_sort(q, part, nparts):
+        if part == 0:
+            st[("xs", q)] = act.tile([P, 4096], BF16, name="xs", tag="xs", bufs=1)
+        raw, xs = st[("raw", q)], st[("xs", q)]
+        na = 8 // nparts
+        src = raw[:].rearrange("p n d -> p (n d)").bitcast(F32).rearrange("p (a q u) -> p a u q", a=8, u=2)
+        dst = xs[:].bitcast(F32).rearrange("p (a u q) -> p a u q", a=8, u=2)
+        nc.scalar.copy(out=dst[:, na * part:na * (part + 1)], in_=src[:, na * part:na * (part + 1)])
+
+    def x_tr(q, ptag, is_sorted):
+        banks = []
+        if is_sorted:
+            words = st.pop(("xs", q))[:].bitcast(F32)
+            st.pop(("raw", q))
+        else:
+            words = st.pop(("raw", q))[:].rearrange("p n d -> p (n d)").bitcast(F32)
+        for gg in range(2):
+            for jh in range(2):
+                tp = psum.tile([P, 512], F32, name=ptag, tag=ptag)
+                for jj in range(2):
+                    for u in range(2):
+                        a = 2 * (2 * jh + jj) + gg
+                        if is_sorted:
+                            src = words[:, (2 * a + u) * 128:(2 * a + u + 1) * 128]
+                        else:
+                            src = words[:, 256 * a + u:256 * (a + 1):2]
+                        nc.tensor.transpose(out=tp[:, (2 * jj + u) * 128:(2 * jj + u + 1) * 128], in_=src, identity=st["ident"][:])
+                banks.append(tp)
+        st[("tp", q)] = banks
+
+    def x_copy(q, k, eng):
+        gg, jh = k // 2, k % 2
+        if jh == 0:
+            st[("xg", q, gg)] = act.tile([P, 2048], BF16, name="grp", tag="grp", bufs=cfg["grp_bufs"], align_bytes=64)
+        gr = st[("xg", q, gg)]
+        tp = st[("tp", q)][k]
+        cp = eng.tensor_copy if eng is nc.vector else eng.copy
+        cp(out=gr[:].bitcast(F32)[:, 512 * jh:512 * (jh + 1)].rearrange("p (jj r u) -> p jj r u", jj=2, u=2),
+           in_=tp[:].rearrange("p (jj u r) -> p jj r u", jj=2, u=2))
+
+    def x_codes(b, g):
+        return st[("xc", b)][g // 4][:, g % 4, :], st[("xp", b)][4 * (g % 4):P, g // 4, :]
+
+    def x_alloc(b, tags):
+        if tags[0][0] == "u":
+            st[("xc", b)] = [wpool.tile([P, 4, 512], U32, name=tg, tag=tg, align_bytes=64) for tg in tags]
+        else:
+            st[("xc", b)] = [act.tile([P, 4, 512], U32, name=tg, tag=tg, bufs=1, align_bytes=64) for tg in tags]
+        st[("xp", b)] = act.tile([P, 2, 512], U8, name="xp", tag="xp", bufs=cfg["xp_bufs"], align_bytes=64)
+
+    def x_quant(q, gg):
+        b, g = q // 4, 2 * (q % 4) + gg
+        cd, pl = x_codes(b, g)
+        nc.vector.quantize_mx(out=cd.bitcast(FP8X4), scales=pl, in_=st.pop(("xg", q, gg))[:])
+
+    def s1_open(b, c, t, ptag):
+        st[("a1", b, c, t)] = psum.tile([P, 512], F32, name=ptag, tag=ptag)
+
+    def s1_mm(b, c, t, g, first, last):
+        wc, wp = w_codes(("down", c, g))
+        cd, pl = x_codes(b, g)
+        nc.tensor.matmul_mx(out=st[("a1", b, c, t)][:], lhsT=wc[:, 128 * t:128 * (t + 1)].bitcast(FP8X4),
+                            lhsT_scale=wp[:, 128 * t:128 * (t + 1)], rhs=cd.bitcast(FP8X4), rhs_scale=pl,
+                            start=first, stop=last)
+
+    def dq_evac(b, c, t, eng):
+        if ("dqb", b, c) not in st:
+            st[("dqb", b, c)] = act.tile([P, 4, 512], BF16, name="dqb", tag="dqb", bufs=2)
+        cp = eng.tensor_copy if eng is nc.vector else eng.copy
+        cp(out=st[("dqb", b, c)][:, t, :], in_=st.pop(("a1", b, c, t))[:])
+
+    def dq_inter(b, c):
+        gr = act.tile([P, 2048], BF16, name="grp", tag="grp", bufs=cfg["grp_bufs"], align_bytes=64)
+        nc.vector.tensor_copy(out=gr[:].rearrange("p (n t) -> p n t", t=4), in_=st.pop(("dqb", b, c))[:].rearrange("p t n -> p n t"))
+        st[("dqg", b, c)] = gr
+
+    def dq_quant(b, c):
+        if c == 0:
+            st[("dqc", b)] = act.tile([P, 4, 512], U32, name="dqc", tag="dqc", bufs=cfg["dq_bufs"], align_bytes=64)
+            st[("dqp", b)] = act.tile([P, 512], U8, name="dqp", tag="dqp", bufs=cfg["dq_bufs"], align_bytes=64)
+        nc.vector.quantize_mx(out=st[("dqc", b)][:, c, :].bitcast(FP8X4), scales=st[("dqp", b)][4 * c:P, :], in_=st.pop(("dqg", b, c))[:])
+
+    def s2_group(b, tt, n, ptag):
+        acc = psum.tile([P, 512], F32, name=ptag, tag=ptag)
+        for g in range(G2):
+            wc, wp = w_codes(("up", n, g))
+            nc.tensor.matmul_mx(out=acc[:], lhsT=st[("dqc", b)][:, g, 128 * tt:128 * (tt + 1)].bitcast(FP8X4),
+                                lhsT_scale=st[("dqp", b)][4 * g:P, 128 * tt:128 * (tt + 1)],
+                                rhs=wc.bitcast(FP8X4), rhs_scale=wp, start=(g == 0), stop=(g == G2 - 1))
+        st[("a2", b, tt, n)] = acc
+
+    def stg_get(b, tt, m):
+        if ("stg", b, tt, m) not in st:
+            st[("stg", b, tt, m)] = late.tile([P, 8, DH + DR], F32, name="stg", tag="stg", bufs=3, offset=0)
+        return st[("stg", b, tt, m)]
+
+    def qc_evac(b, tt, n, eng):
+        sg = stg_get(b, tt, n // 2)
+        cp = eng.tensor_copy if eng is nc.vector else eng.copy
+        cp(out=sg[:, 4 * (n % 2):4 * (n % 2) + 4, 0:DH], in_=st.pop(("a2", b, tt, n))[:].rearrange("p (h f) -> p h f", h=4))
+
+    def rope(b, tt, m):
+        nt = 4 * b + tt
+        sg = stg_get(b, tt, m)
+        acc = st.pop(("a2", b, tt, 4 + m))
+        t1 = late.tile([P, 512], F32, name="t1", tag="t1", bufs=1, offset=18432)
+        t2 = late.tile([P, 512], F32, name="t2", tag="t2", bufs=1, offset=20480)
+        cosb = st["cos"][:, nt, :].unsqueeze(1)
+        nc.vector.tensor_tensor(out=t1[:].rearrange("p (a i) -> p a i", i=HALF), in0=acc[:].rearrange("p (a i) -> p a i", i=HALF),
+                                in1=cosb.to_broadcast([P, 16, HALF]), op=ALU.mult)
+        av = acc[:].rearrange("p (h e i) -> p h e i", e=2, i=HALF)
+        tv = t2[:].rearrange("p (h e i) -> p h e i", e=2, i=HALF)
+        sinb = st["sin"][:, nt, :].unsqueeze(1).to_broadcast([P, 8, HALF])
+        nc.vector.scalar_tensor_tensor(out=tv[:, :, 0, :], in0=av[:, :, 1, :], scalar=-1.0, in1=sinb, op0=ALU.mult, op1=ALU.mult)
+        nc.vector.tensor_tensor(out=tv[:, :, 1, :], in0=av[:, :, 0, :], in1=sinb, op=ALU.mult)
+        nc.vector.tensor_tensor(out=sg[:, :, DH:DH + DR].rearrange("p h (i e) -> p h i e", e=2),
+                                in0=t1[:].rearrange("p (h e i) -> p h i e", e=2, i=HALF),
+                                in1=t2[:].rearrange("p (h e i) -> p h i e", e=2, i=HALF), op=ALU.add)
+
+    def store(b, tt, m):
+        nc.sync.dma_start(out=ov[4 * b + tt][:, 8 * m:8 * m + 8, :], in_=st.pop(("stg", b, tt, m))[:])
+
+
+    V, A = nc.vector, nc.scalar
+    FS = cfg["first_sorted"]
+    NQ = 4 * NB
+
+    units = [("down", c, g) for c in range(4) for g in range(G1)] + [("up", n, g) for n in (0, 1, 4, 2, 3, 5) for g in range(G2)]
+    ws = {"load": 0, "next": 0, "lag": None, "xload": 0}
+
+    def w_prefetch():
+        while ws["load"] < len(units) and ws["load"] < ws["next"] + (4 if ws["load"] >= 32 else (8 if ws["next"] < 8 else 12)):
+            w_load(ws["load"] // 2, units[ws["load"]], units[ws["load"] + 1])
+            ws["load"] += 2
+
+    def w_pair(mid):
+        a, b = units[ws["next"]], units[ws["next"] + 1]
+        ws["next"] += 2
+        w_inter(a, A)
+        w_inter(b, V)
+        w_prefetch()
+        w_quant(b)
+        if mid is not None:
+            mid()
+        w_quant(a)
+
+    def need_pairs(n):
+        while ws["next"] < 2 * n:
+            w_pair(None)
+
+    def bg_pair(limit):
+        if ws["next"] < 2 * limit:
+            w_pair(None)
+
+    def x_prefetch(limit):
+        while ws["xload"] < min(limit, NQ):
+            x_load(ws["xload"])
+            ws["xload"] += 1
+
+    pend = []
+
+    def run_pend():
+        while pend:
+            pend.pop(0)()
+
+    def dq_finish(b, c):
+        dq_inter(b, c)
+        dq_quant(b, c)
+
+    def chunk_out(b, c):
+        for t in range(4):
+            dq_evac(b, c, t, A if t % 2 == 0 else V)
+        dq_finish(b, c)
+
+    prog = {}
+
+    def s1_pass(b, c, g, ptag):
+        n = prog.get((b, c), 0)
+        for t in range(4):
+            if n == 0:
+                s1_open(b, c, t, ptag)
+            s1_mm(b, c, t, g, n == 0, n == G1 - 1)
+        prog[(b, c)] = n + 1
+        if n == G1 - 1:
+            pend.append(lambda: chunk_out(b, c))
+
+    def s1_group(b, c, t, ptag):
+        s1_open(b, c, t, ptag)
+        for g in range(G1):
+            s1_mm(b, c, t, g, g == 0, g == G1 - 1)
+        run_pend()
+        dq_evac(b, c, t, A)
+        if t == 3:
+            pend.append(lambda: dq_finish(b, c))
+
+    def x_tr_head(q):
+        x_tr(q, "tp", q >= 4 * FS)
+        if q < 4 * FS:
+            x_prefetch(q + 5 if q <= 6 else (q + 4 if q <= 9 else q + 3))
+
+    def x_copies_head(q):
+        if q % 4 == 0:
+            x_alloc(q // 4, ("up3c0", "up5c0") if q // 4 == 1 else ("xc0", "xc1"))
+        for k in range(4):
+            x_copy(q, k, A)
+
+    def x_quants(q):
+        x_quant(q, 0)
+        x_quant(q, 1)
+
+    def half_chunk(b, c, h, ptag):
+        need_pairs(4 * c + 2 * h + 2)
+        for g in range(4 * h, 4 * h + 4):
+            s1_pass(b, c, g, ptag)
+
+    setup()
+    for k in range(4):
+        x_prefetch(k + 1)
+        ws["next"] = 2 * k - 6
+        w_prefetch()
+    ws["next"] = 0
+
+    x_tr_head(0)
+    for q in range(8):
+        x_copies_head(q)
+        if q + 1 < 8:
+            x_tr_head(q + 1)
+        if q < 4 or q % 2 == 1:
+            w_pair(lambda: x_quants(q))
+        else:
+            x_quants(q)
+        run_pend()
+        if q % 2 == 1:
+            half_chunk(q // 4, 0, (q % 4) // 2, "acc")
+    for c in range(1, 4):
+        for h in range(2):
+            half_chunk(0, c, h, "tp")
+            bg_pair(28)
+            run_pend()
+            half_chunk(1, c, h, "acc")
+            bg_pair(28)
+            run_pend()
+    x_tr_head(8)
+    for q in range(8, 12):
+        x_copies_head(q)
+        if q + 1 < 12:
+            x_tr_head(q + 1)
+        w_pair(lambda: x_quants(q))
+        run_pend()
+        if q % 2 == 1:
+            half_chunk(2, 0, (q % 4) // 2, "acc")
+    x_sort(12, 0, 1)
+    run_pend()
+    x_prefetch(15)
+    tables()
+    for c in range(1, 4):
+        for t in range(4):
+            s1_group(2, c, t, "acc")
+            if t % 2 == 0:
+                bg_pair(28)
+    run_pend()
+
+    def a_step(i, r, q):
+        nxt = None
+        if q is not None:
+            if r == 0:
+                x_alloc(q // 4, ("xc0", "xc1"))
+            x_tr(q, "tp", True)
+            x_copy(q, 0, V)
+            x_copy(q, 1, A)
+            x_copy(q, 2, V)
+            x_copy(q, 3, A)
+            if q + 1 < NQ:
+                nxt = q + 1
+        if nxt is not None:
+            x_sort(nxt, 0, 2)
+        s2_group(i, r, 0, "acc")
+        if q is not None:
+            x_quant(q, 0)
+        qc_evac(i, r, 0, A)
+        s2_group(i, r, 1, "acc")
+        if q is not None:
+            x_quant(q, 1)
+        if nxt is not None:
+            x_sort(nxt, 1, 2)
+            x_prefetch(nxt + 3)
+        qc_evac(i, r, 1, A)
+        s2_group(i, r, 4, "acc")
+        rope(i, r, 0)
+        store(i, r, 0)
+        s2_group(i, r, 2, "acc")
+        qc_evac(i, r, 2, A)
+        s2_group(i, r, 3, "acc")
+        qc_evac(i, r, 3, A)
+        s2_group(i, r, 5, "acc")
+        rope(i, r, 1)
+        store(i, r, 1)
+
+    for i in range(NB):
+        b = i + 3
+        for r in range(4):
+            a_step(i, r, 4 * b + r if b < NB else None)
+        if b < NB:
+            for c in range(4):
+                for t in range(4):
+                    s1_group(b, c, t, "acc")
+            run_pend()
+
+
+def tile_multiheadlatentattention_pa_l_kernel(tc, x, W_q_down, W_q_up, W_q_rope, rope_cos, rope_sin, out):
+    with ExitStack() as ctx:
+        build(tc, x, W_q_down, W_q_up, W_q_rope, rope_cos, rope_sin, out, ctx,
+              {"grp_bufs": 4, "xp_bufs": 2, "dq_bufs": 3, "first_sorted": 3, "h5_every": 2})

@@ -301,7 +301,7 @@ def build(tc, x, W_q_down, W_q_up, W_q_rope, rope_cos, rope_sin, out, ctx, cfg):
         for g in range(G1):
             s1_mm(b, c, t, g, g == 0, g == G1 - 1)
         run_pend()
-        dq_evac(b, c, t, A)
+        dq_evac(b, c, t, V if (b >= 3 and t % 2 == 1) else A)
         if t == 3:
             pend.append(lambda: dq_finish(b, c))
 
@@ -332,21 +332,32 @@ def build(tc, x, W_q_down, W_q_up, W_q_rope, rope_cos, rope_sin, out, ctx, cfg):
         w_prefetch()
     ws["next"] = 0
 
-    x_tr_head(0)
-    for q in range(8):
+    lag = []
+
+    def run_lag():
+        while lag:
+            lag.pop(0)()
+
+    def t_and_p(q, last, with_pair):
         x_copies_head(q)
-        if q + 1 < 8:
+        if q + 1 < last:
             x_tr_head(q + 1)
-        if q < 4 or q % 2 == 1:
+        run_lag()
+        if with_pair:
             w_pair(lambda: x_quants(q))
         else:
             x_quants(q)
         run_pend()
         if q % 2 == 1:
-            half_chunk(q // 4, 0, (q % 4) // 2, "acc")
+            lag.append(lambda: half_chunk(q // 4, 0, (q % 4) // 2, "acc"))
+
+    x_tr_head(0)
+    for q in range(8):
+        t_and_p(q, 8, q < 4 or q % 2 == 1)
     for c in range(1, 4):
         for h in range(2):
             half_chunk(0, c, h, "tp")
+            run_lag()
             bg_pair(28)
             run_pend()
             half_chunk(1, c, h, "acc")
@@ -354,21 +365,16 @@ def build(tc, x, W_q_down, W_q_up, W_q_rope, rope_cos, rope_sin, out, ctx, cfg):
             run_pend()
     x_tr_head(8)
     for q in range(8, 12):
-        x_copies_head(q)
-        if q + 1 < 12:
-            x_tr_head(q + 1)
-        w_pair(lambda: x_quants(q))
-        run_pend()
-        if q % 2 == 1:
-            half_chunk(2, 0, (q % 4) // 2, "acc")
+        t_and_p(q, 12, q % 2 == 1)
     x_sort(12, 0, 1)
-    run_pend()
     x_prefetch(15)
     tables()
+    run_lag()
+    run_pend()
     for c in range(1, 4):
         for t in range(4):
             s1_group(2, c, t, "acc")
-            if t % 2 == 0:
+            if t != 3:
                 bg_pair(28)
     run_pend()
 
@@ -386,29 +392,28 @@ def build(tc, x, W_q_down, W_q_up, W_q_rope, rope_cos, rope_sin, out, ctx, cfg):
                 nxt = q + 1
         if nxt is not None:
             x_sort(nxt, 0, 2)
-        s2_group(i, r, 0, "acc")
+        s2_group(i, r, 4, "acc")
         if q is not None:
             x_quant(q, 0)
-        qc_evac(i, r, 0, A)
-        s2_group(i, r, 1, "acc")
-        if q is not None:
             x_quant(q, 1)
+        rope(i, r, 0)
+        s2_group(i, r, 0, "acc")
+        qc_evac(i, r, 0, A)
         if nxt is not None:
             x_sort(nxt, 1, 2)
             x_prefetch(nxt + 3)
+        s2_group(i, r, 1, "acc")
         qc_evac(i, r, 1, A)
-        s2_group(i, r, 4, "acc")
-        rope(i, r, 0)
         store(i, r, 0)
+        s2_group(i, r, 5, "acc")
+        rope(i, r, 1)
         s2_group(i, r, 2, "acc")
         qc_evac(i, r, 2, A)
         s2_group(i, r, 3, "acc")
         qc_evac(i, r, 3, A)
-        s2_group(i, r, 5, "acc")
-        rope(i, r, 1)
         store(i, r, 1)
 
-    for i in range(NB):
+    for i in range(cfg["nsteady"]):
         b = i + 3
         for r in range(4):
             a_step(i, r, 4 * b + r if b < NB else None)
@@ -422,4 +427,4 @@ def build(tc, x, W_q_down, W_q_up, W_q_rope, rope_cos, rope_sin, out, ctx, cfg):
 def tile_multiheadlatentattention_pa_l_kernel(tc, x, W_q_down, W_q_up, W_q_rope, rope_cos, rope_sin, out):
     with ExitStack() as ctx:
         build(tc, x, W_q_down, W_q_up, W_q_rope, rope_cos, rope_sin, out, ctx,
-              {"grp_bufs": 4, "xp_bufs": 2, "dq_bufs": 3, "first_sorted": 3, "h5_every": 2})
+              {"grp_bufs": 4, "xp_bufs": 2, "dq_bufs": 3, "first_sorted": 3, "h5_every": 2, "nsteady": NB})

@@ -332,24 +332,20 @@ def build(tc, x, W_q_down, W_q_up, W_q_rope, rope_cos, rope_sin, out, ctx, cfg):
         w_prefetch()
     ws["next"] = 0
 
-    lag = []
-
-    def run_lag():
-        while lag:
-            lag.pop(0)()
+    def run_passes(q):
+        for g in (2 * (q % 4), 2 * (q % 4) + 1):
+            s1_pass(q // 4, 0, g, "acc")
 
     def t_and_p(q, last, with_pair):
         x_copies_head(q)
         if q + 1 < last:
             x_tr_head(q + 1)
-        run_lag()
         if with_pair:
             w_pair(lambda: x_quants(q))
         else:
             x_quants(q)
         run_pend()
-        if q % 2 == 1:
-            lag.append(lambda: half_chunk(q // 4, 0, (q % 4) // 2, "acc"))
+        run_passes(q)
 
     x_tr_head(0)
     for q in range(8):
@@ -357,19 +353,23 @@ def build(tc, x, W_q_down, W_q_up, W_q_rope, rope_cos, rope_sin, out, ctx, cfg):
     for c in range(1, 4):
         for h in range(2):
             half_chunk(0, c, h, "tp")
-            run_lag()
             bg_pair(28)
             run_pend()
-            half_chunk(1, c, h, "acc")
-            bg_pair(28)
-            run_pend()
+            if (c, h) != (3, 1):
+                half_chunk(1, c, h, "acc")
+                bg_pair(28)
+                run_pend()
+    s1_pass(1, 3, 4, "acc")
+    s1_pass(1, 3, 5, "acc")
     x_tr_head(8)
+    s1_pass(1, 3, 6, "acc")
+    s1_pass(1, 3, 7, "acc")
+    bg_pair(28)
     for q in range(8, 12):
         t_and_p(q, 12, q % 2 == 1)
     x_sort(12, 0, 1)
     x_prefetch(15)
     tables()
-    run_lag()
     run_pend()
     for c in range(1, 4):
         for t in range(4):

@@ -23,7 +23,6 @@ FLOPS = 2 * S * D * DQ + 2 * S * DQ * (H * DH + H * DR)
 
 def build(tc, x, W_q_down, W_q_up, W_q_rope, rope_cos, rope_sin, out, ctx, cfg):
     nc = tc.nc
-    ctx.enter_context(tc.manual_schedule())
     const = ctx.enter_context(tc.tile_pool(name="const", bufs=1))
     wpool = ctx.enter_context(tc.tile_pool(name="wts", bufs=1))
     act = ctx.enter_context(tc.tile_pool(name="act", bufs=2))

@@ -300,7 +300,7 @@ def build(tc, x, W_q_down, W_q_up, W_q_rope, rope_cos, rope_sin, out, ctx, cfg):
         for g in range(G1):
             s1_mm(b, c, t, g, g == 0, g == G1 - 1)
         run_pend()
-        dq_evac(b, c, t, V if (b >= 3 and t % 2 == 1) else A)
+        dq_evac(b, c, t, A)
         if t == 3:
             pend.append(lambda: dq_finish(b, c))
 

from contextlib import ExitStack

import concourse.mybir as mybir
from concourse.masks import make_identity

F32 = mybir.dt.float32
BF16 = mybir.dt.bfloat16
U32 = mybir.dt.uint32
U8 = mybir.dt.uint8
FP8X4 = mybir.dt.float8_e4m3fn_x4
ALU = mybir.AluOpType

P = 128
S, D, DQ = 4096, 4096, 2048
H, DH, DR = 16, 128, 64
HALF = DR // 2
NT = S // P
NB = 8
G1 = D // 512
G2 = DQ // 512
FLOPS = 2 * S * D * DQ + 2 * S * DQ * (H * DH + H * DR)


def build(tc, x, W_q_down, W_q_up, W_q_rope, rope_cos, rope_sin, out, ctx, cfg):
    nc = tc.nc
    const = ctx.enter_context(tc.tile_pool(name="const", bufs=1))
    wpool = ctx.enter_context(tc.tile_pool(name="wts", bufs=1))
    act = ctx.enter_context(tc.tile_pool(name="act", bufs=2))
    late = ctx.enter_context(tc.tile_pool(name="late", bufs=2))
    psum = ctx.enter_context(tc.psum_pool(name="psum", bufs=4))

    xv = x[0].rearrange("(p n) d -> p n d", n=NT)
    ov = out[0].rearrange("h (p n) f -> n p h f", n=NT)
    st = {}

    def setup():
        ident = const.tile([P, P], F32, name="ident", tag="ident")
        make_identity(nc, ident[:])
        st["ident"] = ident

    def tables():
        cos = const.tile([P, NT, HALF], BF16, name="cos", tag="cos")
        sin = const.tile([P, NT, HALF], BF16, name="sin", tag="sin")
        nc.sync.dma_start(out=cos[:], in_=rope_cos.rearrange("(p n) i -> p n i", n=NT))
        nc.sync.dma_start(out=sin[:], in_=rope_sin.rearrange("(p n) i -> p n i", n=NT))
        st["cos"], st["sin"] = cos, sin

    def w_src(u):
        kind, c, g = u
        if kind == "down":
            w = W_q_down[512 * g:512 * (g + 1), 512 * c:512 * (c + 1)]
        elif c < 4:
            w = W_q_up[512 * g:512 * (g + 1), 512 * c:512 * (c + 1)]
        else:
            w = W_q_rope[512 * g:512 * (g + 1), 512 * (c - 4):512 * (c - 3)]
        return w.rearrange("(p j) w -> p j w", j=4)

    def w_load(pi, ua, ub):
        tg = ("up0c0", "up1c0", "up4c0", "up2c0", "wraw", "wraw")[pi % 6] if pi < 16 else "wraw"
        if tg == "wraw":
            wr = late.tile([P, 2, 4, 512], BF16, name="wraw", tag="wraw", bufs=2, offset=0)
        else:
            wr = wpool.tile([P, 2, 4, 512], BF16, name=tg, tag=tg, align_bytes=64)
        nc.sync.dma_start(out=wr[:, 0], in_=w_src(ua))
        nc.sync.dma_start(out=wr[:, 1], in_=w_src(ub))
        st[("wraw", ua)] = wr[:, 0]
        st[("wraw", ub)] = wr[:, 1]

    def w_inter(u, eng):
        kind, c, g = u
        wr = st.pop(("wraw", u))
        gr = act.tile([P, 2048], BF16, name="grp", tag="grp", bufs=cfg["grp_bufs"], align_bytes=64)
        cp = eng.tensor_copy if eng is nc.vector else eng.copy
        if kind == "down":
            cp(out=gr[:].rearrange("p (t m j) -> p t m j", t=4, j=4), in_=wr.rearrange("p j (m t) -> p t m j", t=4))
        elif c < 4:
            cp(out=gr[:].rearrange("p (w j) -> p w j", j=4), in_=wr.rearrange("p j w -> p w j"))
        else:
            go = gr[:].rearrange("p (h e i j) -> p h e i j", h=8, e=2, j=4)
            wi = wr.rearrange("p j (h i e) -> p h e i j", h=8, e=2)
            for e in range(2):
                cp(out=go[:, :, e], in_=wi[:, :, e])
        st[("wgrp", u)] = gr

    def w_codes(u):
        kind, c, g = u
        key = (kind, c)
        if key not in st:
            ng = G1 if kind == "down" else G2
            nm = "%s%d" % (kind, c)
            st[key] = [wpool.tile([P, 4, 512], U32, name="%sc%d" % (nm, q), tag="%sc%d" % (nm, q), align_bytes=64) for q in range(ng // 4)]
            st[(kind, c, "pl")] = [wpool.tile([P, 512], U8, name="%sp%d" % (nm, q), tag="%sp%d" % (nm, q), align_bytes=64) for q in range(ng // 4)]
        return st[key][g // 4][:, g % 4, :], st[(kind, c, "pl")][g // 4][4 * (g % 4):P, :]

    def w_quant(u):
        gr = st.pop(("wgrp", u))
        cd, pl = w_codes(u)
        nc.vector.quantize_mx(out=cd.bitcast(FP8X4), scales=pl, in_=gr[:])

    def x_load(q):
        b, r = q // 4, q % 4
        tg = ("raw", "raw", "xs", "dqc")[q % 4] if q < 8 else ("xs" if q == 10 else "raw")
        if tg == "raw":
            raw = act.tile([P, 4, 1024], BF16, name="raw", tag="raw", bufs=2)
        elif tg == "xs":
            raw = act.tile([P, 4, 1024], BF16, name="xs", tag="xs", bufs=1)
        else:
            raw = act.tile([P, 4, 1024], BF16, name="dqc", tag="dqc", bufs=cfg["dq_bufs"], align_bytes=64)
        nc.sync.dma_start(out=raw[:], in_=xv[:, 4 * b:4 * b + 4, 1024 * r:1024 * (r + 1)])
        st[("raw", q)] = raw

    def x_sort(q, part, nparts):
        if part == 0:
            st[("xs", q)] = act.tile([P, 4096], BF16, name="xs", tag="xs", bufs=1)
        raw, xs = st[("raw", q)], st[("xs", q)]
        na = 8 // nparts
        src = raw[:].rearrange("p n d -> p (n d)").bitcast(F32).rearrange("p (a q u) -> p a u q", a=8, u=2)
        dst = xs[:].bitcast(F32).rearrange("p (a u q) -> p a u q", a=8, u=2)
        nc.scalar.copy(out=dst[:, na * part:na * (part + 1)], in_=src[:, na * part:na * (part + 1)])

    def x_tr(q, ptag, is_sorted):
        banks = []
        if is_sorted:
            words = st.pop(("xs", q))[:].bitcast(F32)
            st.pop(("raw", q))
        else:
            words = st.pop(("raw", q))[:].rearrange("p n d -> p (n d)").bitcast(F32)
        for gg in range(2):
            for jh in range(2):
                tp = psum.tile([P, 512], F32, name=ptag, tag=ptag)
                for jj in range(2):
                    for u in range(2):
                        a = 2 * (2 * jh + jj) + gg
                        if is_sorted:
                            src = words[:, (2 * a + u) * 128:(2 * a + u + 1) * 128]
                        else:
                            src = words[:, 256 * a + u:256 * (a + 1):2]
                        nc.tensor.transpose(out=tp[:, (2 * jj + u) * 128:(2 * jj + u + 1) * 128], in_=src, identity=st["ident"][:])
                banks.append(tp)
        st[("tp", q)] = banks

    def x_copy(q, k, eng):
        gg, jh = k // 2, k % 2
        if jh == 0:
            st[("xg", q, gg)] = act.tile([P, 2048], BF16, name="grp", tag="grp", bufs=cfg["grp_bufs"], align_bytes=64)
        gr = st[("xg", q, gg)]
        tp = st[("tp", q)][k]
        cp = eng.tensor_copy if eng is nc.vector else eng.copy
        cp(out=gr[:].bitcast(F32)[:, 512 * jh:512 * (jh + 1)].rearrange("p (jj r u) -> p jj r u", jj=2, u=2),
           in_=tp[:].rearrange("p (jj u r) -> p jj r u", jj=2, u=2))

    def x_codes(b, g):
        return st[("xc", b)][g // 4][:, g % 4, :], st[("xp", b)][4 * (g % 4):P, g // 4, :]

    def x_alloc(b, tags):
        if tags[0][0] == "u":
            st[("xc", b)] = [wpool.tile([P, 4, 512], U32, name=tg, tag=tg, align_bytes=64) for tg in tags]
        else:
            st[("xc", b)] = [act.tile([P, 4, 512], U32, name=tg, tag=tg, bufs=1, align_bytes=64) for tg in tags]
        st[("xp", b)] = act.tile([P, 2, 512], U8, name="xp", tag="xp", bufs=cfg["xp_bufs"], align_bytes=64)

    def x_quant(q, gg):
        b, g = q // 4, 2 * (q % 4) + gg
        cd, pl = x_codes(b, g)
        nc.vector.quantize_mx(out=cd.bitcast(FP8X4), scales=pl, in_=st.pop(("xg", q, gg))[:])

    def s1_open(b, c, t, ptag):
        st[("a1", b, c, t)] = psum.tile([P, 512], F32, name=ptag, tag=ptag)

    def s1_mm(b, c, t, g, first, last):
        wc, wp = w_codes(("down", c, g))
        cd, pl = x_codes(b, g)
        nc.tensor.matmul_mx(out=st[("a1", b, c, t)][:], lhsT=wc[:, 128 * t:128 * (t + 1)].bitcast(FP8X4),
                            lhsT_scale=wp[:, 128 * t:128 * (t + 1)], rhs=cd.bitcast(FP8X4), rhs_scale=pl,
                            start=first, stop=last)

    def dq_evac(b, c, t, eng):
        if ("dqb", b, c) not in st:
            st[("dqb", b, c)] = act.tile([P, 4, 512], BF16, name="dqb", tag="dqb", bufs=2)
        cp = eng.tensor_copy if eng is nc.vector else eng.copy
        cp(out=st[("dqb", b, c)][:, t, :], in_=st.pop(("a1", b, c, t))[:])

    def dq_inter(b, c):
        gr = act.tile([P, 2048], BF16, name="grp", tag="grp", bufs=cfg["grp_bufs"], align_bytes=64)
        nc.vector.tensor_copy(out=gr[:].rearrange("p (n t) -> p n t", t=4), in_=st.pop(("dqb", b, c))[:].rearrange("p t n -> p n t"))
        st[("dqg", b, c)] = gr

    def dq_quant(b, c):
        if c == 0:
            st[("dqc", b)] = act.tile([P, 4, 512], U32, name="dqc", tag="dqc", bufs=cfg["dq_bufs"], align_bytes=64)
            st[("dqp", b)] = act.tile([P, 512], U8, name="dqp", tag="dqp", bufs=cfg["dq_bufs"], align_bytes=64)
        nc.vector.quantize_mx(out=st[("dqc", b)][:, c, :].bitcast(FP8X4), scales=st[("dqp", b)][4 * c:P, :], in_=st.pop(("dqg", b, c))[:])

    def s2_group(b, tt, n, ptag):
        acc = psum.tile([P, 512], F32, name=ptag, tag=ptag)
        for g in range(G2):
            wc, wp = w_codes(("up", n, g))
            nc.tensor.matmul_mx(out=acc[:], lhsT=st[("dqc", b)][:, g, 128 * tt:128 * (tt + 1)].bitcast(FP8X4),
                                lhsT_scale=st[("dqp", b)][4 * g:P, 128 * tt:128 * (tt + 1)],
                                rhs=wc.bitcast(FP8X4), rhs_scale=wp, start=(g == 0), stop=(g == G2 - 1))
        st[("a2", b, tt, n)] = acc

    def stg_get(b, tt, m):
        if ("stg", b, tt, m) not in st:
            st[("stg", b, tt, m)] = late.tile([P, 8, DH + DR], F32, name="stg", tag="stg", bufs=3, offset=0)
        return st[("stg", b, tt, m)]

    def qc_evac(b, tt, n, eng):
        sg = stg_get(b, tt, n // 2)
        cp = eng.tensor_copy if eng is nc.vector else eng.copy
        cp(out=sg[:, 4 * (n % 2):4 * (n % 2) + 4, 0:DH], in_=st.pop(("a2", b, tt, n))[:].rearrange("p (h f) -> p h f", h=4))

    def rope(b, tt, m):
        nt = 4 * b + tt
        sg = stg_get(b, tt, m)
        acc = st.pop(("a2", b, tt, 4 + m))
        t1 = late.tile([P, 512], F32, name="t1", tag="t1", bufs=1, offset=18432)
        t2 = late.tile([P, 512], F32, name="t2", tag="t2", bufs=1, offset=20480)
        cosb = st["cos"][:, nt, :].unsqueeze(1)
        nc.vector.tensor_tensor(out=t1[:].rearrange("p (a i) -> p a i", i=HALF), in0=acc[:].rearrange("p (a i) -> p a i", i=HALF),
                                in1=cosb.to_broadcast([P, 16, HALF]), op=ALU.mult)
        av = acc[:].rearrange("p (h e i) -> p h e i", e=2, i=HALF)
        tv = t2[:].rearrange("p (h e i) -> p h e i", e=2, i=HALF)
        sinb = st["sin"][:, nt, :].unsqueeze(1).to_broadcast([P, 8, HALF])
        nc.vector.scalar_tensor_tensor(out=tv[:, :, 0, :], in0=av[:, :, 1, :], scalar=-1.0, in1=sinb, op0=ALU.mult, op1=ALU.mult)
        nc.vector.tensor_tensor(out=tv[:, :, 1, :], in0=av[:, :, 0, :], in1=sinb, op=ALU.mult)
        nc.vector.tensor_tensor(out=sg[:, :, DH:DH + DR].rearrange("p h (i e) -> p h i e", e=2),
                                in0=t1[:].rearrange("p (h e i) -> p h i e", e=2, i=HALF),
                                in1=t2[:].rearrange("p (h e i) -> p h i e", e=2, i=HALF), op=ALU.add)

    def store(b, tt, m):
        nc.sync.dma_start(out=ov[4 * b + tt][:, 8 * m:8 * m + 8, :], in_=st.pop(("stg", b, tt, m))[:])


    V, A = nc.vector, nc.scalar
    FS = cfg["first_sorted"]
    NQ = 4 * NB

    units = [("down", c, g) for c in range(4) for g in range(G1)] + [("up", n, g) for n in (0, 1, 4, 2, 3, 5) for g in range(G2)]
    ws = {"load": 0, "next": 0, "lag": None, "xload": 0}

    def w_prefetch():
        while ws["load"] < len(units) and ws["load"] < ws["next"] + (4 if ws["load"] >= 32 else (8 if ws["next"] < 8 else 12)):
            w_load(ws["load"] // 2, units[ws["load"]], units[ws["load"] + 1])
            ws["load"] += 2

    def w_pair(mid):
        a, b = units[ws["next"]], units[ws["next"] + 1]
        ws["next"] += 2
        w_inter(a, A)
        w_inter(b, V)
        w_prefetch()
        w_quant(b)
        if mid is not None:
            mid()
        w_quant(a)

    def need_pairs(n):
        while ws["next"] < 2 * n:
            w_pair(None)

    def bg_pair(limit):
        if ws["next"] < 2 * limit:
            w_pair(None)

    def x_prefetch(limit):
        while ws["xload"] < min(limit, NQ):
            x_load(ws["xload"])
            ws["xload"] += 1

    pend = []

    def run_pend():
        while pend:
            pend.pop(0)()

    def dq_finish(b, c):
        dq_inter(b, c)
        dq_quant(b, c)

    def chunk_out(b, c):
        for t in range(4):
            dq_evac(b, c, t, A if t % 2 == 0 else V)
        dq_finish(b, c)

    prog = {}

    def s1_pass(b, c, g, ptag):
        n = prog.get((b, c), 0)
        for t in range(4):
            if n == 0:
                s1_open(b, c, t, ptag)
            s1_mm(b, c, t, g, n == 0, n == G1 - 1)
        prog[(b, c)] = n + 1
        if n == G1 - 1:
            pend.append(lambda: chunk_out(b, c))

    def s1_group(b, c, t, ptag):
        s1_open(b, c, t, ptag)
        for g in range(G1):
            s1_mm(b, c, t, g, g == 0, g == G1 - 1)
        run_pend()
        dq_evac(b, c, t, A)
        if t == 3:
            pend.append(lambda: dq_finish(b, c))

    def x_tr_head(q):
        x_tr(q, "tp", q >= 4 * FS)
        if q < 4 * FS:
            x_prefetch(q + 5 if q <= 6 else (q + 4 if q <= 9 else q + 3))

    def x_copies_head(q):
        if q % 4 == 0:
            x_alloc(q // 4, ("up3c0", "up5c0") if q // 4 == 1 else ("xc0", "xc1"))
        for k in range(4):
            x_copy(q, k, A)

    def x_quants(q):
        x_quant(q, 0)
        x_quant(q, 1)

    def half_chunk(b, c, h, ptag):
        need_pairs(4 * c + 2 * h + 2)
        for g in range(4 * h, 4 * h + 4):
            s1_pass(b, c, g, ptag)

    setup()
    for k in range(4):
        x_prefetch(k + 1)
        ws["next"] = 2 * k - 6
        w_prefetch()
    ws["next"] = 0

    def run_passes(q):
        for g in (2 * (q % 4), 2 * (q % 4) + 1):
            s1_pass(q // 4, 0, g, "acc")

    def t_and_p(q, last, with_pair):
        x_copies_head(q)
        if q + 1 < last:
            x_tr_head(q + 1)
        if with_pair:
            w_pair(lambda: x_quants(q))
        else:
            x_quants(q)
        run_pend()
        run_passes(q)

    x_tr_head(0)
    for q in range(8):
        t_and_p(q, 8, q < 4 or q % 2 == 1)
    for c in range(1, 4):
        for h in range(2):
            half_chunk(0, c, h, "tp")
            bg_pair(28)
            run_pend()
            if (c, h) != (3, 1):
                half_chunk(1, c, h, "acc")
                bg_pair(28)
                run_pend()
    s1_pass(1, 3, 4, "acc")
    s1_pass(1, 3, 5, "acc")
    x_tr_head(8)
    s1_pass(1, 3, 6, "acc")
    s1_pass(1, 3, 7, "acc")
    bg_pair(28)
    for q in range(8, 12):
        t_and_p(q, 12, q % 2 == 1)
    x_sort(12, 0, 1)
    x_prefetch(15)
    tables()
    run_pend()
    for c in range(1, 4):
        for t in range(4):
            s1_group(2, c, t, "acc")
            if t != 3:
                bg_pair(28)
    run_pend()

    def a_step(i, r, q):
        nxt = None
        if q is not None:
            if r == 0:
                x_alloc(q // 4, ("xc0", "xc1"))
            x_tr(q, "tp", True)
            x_copy(q, 0, V)
            x_copy(q, 1, A)
            x_copy(q, 2, V)
            x_copy(q, 3, A)
            if q + 1 < NQ:
                nxt = q + 1
        if nxt is not None:
            x_sort(nxt, 0, 2)
        s2_group(i, r, 4, "acc")
        if q is not None:
            x_quant(q, 0)
            x_quant(q, 1)
        rope(i, r, 0)
        s2_group(i, r, 0, "acc")
        qc_evac(i, r, 0, A)
        if nxt is not None:
            x_sort(nxt, 1, 2)
            x_prefetch(nxt + 3)
        s2_group(i, r, 1, "acc")
        qc_evac(i, r, 1, A)
        store(i, r, 0)
        s2_group(i, r, 5, "acc")
        rope(i, r, 1)
        s2_group(i, r, 2, "acc")
        qc_evac(i, r, 2, A)
        s2_group(i, r, 3, "acc")
        qc_evac(i, r, 3, A)
        store(i, r, 1)

    for i in range(cfg["nsteady"]):
        b = i + 3
        for r in range(4):
            a_step(i, r, 4 * b + r if b < NB else None)
        if b < NB:
            for c in range(4):
                for t in range(4):
                    s1_group(b, c, t, "acc")
            run_pend()


def tile_multiheadlatentattention_pa_l_kernel(tc, x, W_q_down, W_q_up, W_q_rope, rope_cos, rope_sin, out):
    with ExitStack() as ctx:
        build(tc, x, W_q_down, W_q_up, W_q_rope, rope_cos, rope_sin, out, ctx,
              {"grp_bufs": 4, "xp_bufs": 2, "dq_bufs": 3, "first_sorted": 3, "h5_every": 2, "nsteady": NB})
